import numpy as np
import ml_dtypes


def mxq(x, axis, fmt="e4m3"):
    dtype, down = {"e4m3": (ml_dtypes.float8_e4m3fn, 7), "e5m2": (ml_dtypes.float8_e5m2, 14)}[fmt]
    v = np.moveaxis(np.asarray(x, np.float32).astype(ml_dtypes.bfloat16).astype(np.float64), axis, -1)
    blocks = v.reshape(v.shape[:-1] + (-1, 32))
    amax = np.abs(blocks).max(-1, keepdims=True)
    byte = np.maximum(np.where(amax > 0, np.frexp(amax)[1] - 1 + 127, 0) - down, 1)
    scale = np.exp2(byte - 127.0)
    codes = (blocks / scale).astype(np.float32).astype(dtype).astype(np.float64)
    return np.moveaxis((codes * scale).reshape(v.shape), -1, axis)


WIDE = False


def mx_kscale(k):
    if not WIDE:
        return np.ones(k)
    levels = np.array([20, -20, 10, -10, 0])
    a = np.random.permutation(np.resize(levels, k // 512 * 4)).reshape(k // 512, 4)
    idx = np.arange(k)
    return np.exp2(a[idx // 512, idx % 128 // 32])


BF16 = ml_dtypes.bfloat16


def bf(x):
    return np.asarray(x, np.float32).astype(BF16)


def f64(x):
    return np.asarray(x).astype(np.float64)


B, M, F, U = 512, 8, 512, 512


def setup_inputs():
    s = mx_kscale(B)
    limit = np.sqrt(6.0 / (F + U))
    x0 = bf(np.random.standard_normal((B, M, F)))
    W = bf(np.random.uniform(-limit, limit, (M, F, U)))
    b = bf(np.random.standard_normal((M, U)) * 0.1)
    g = bf(np.random.standard_normal((B, M * U)) * np.exp2(np.random.randint(-12, 1, (B, 1))) / s[:, None])
    z = (f64(x0).transpose(1, 0, 2) @ f64(W)).transpose(1, 0, 2) + f64(b)[None, :, :]
    return {"x": bf(f64(x0) * s[:, None, None]), "W": W, "b": b,
            "z": np.asarray(z, np.float32), "grad_out": g}


def reference(x, W, b, z, grad_out):
    dz = f64(grad_out).reshape(B, M, U) * (f64(z) > 0.0)
    xq = mxq(f64(x), 0, "e4m3")
    gq = mxq(dz, 0, "e5m2")
    return xq.transpose(1, 2, 0) @ gq.transpose(1, 0, 2)

@@ -1,0 +1,117 @@
+from contextlib import ExitStack
+
+import concourse.mybir as mybir
+
+F32 = mybir.dt.float32
+BF16 = mybir.dt.bfloat16
+U32 = mybir.dt.uint32
+U8 = mybir.dt.uint8
+E4M3_X4 = mybir.dt.float8_e4m3fn_x4
+E5M2_X4 = mybir.dt.float8_e5m2_x4
+ALU = mybir.AluOpType
+
+P = 128
+PACK = 4
+BATCH, MASKS, F_IN, U_OUT = 512, 8, 512, 512
+assert BATCH == P * PACK
+F_TILES = F_IN // P
+X_MASKS = 4
+Z_MASKS = 2
+
+FLOPS = 2 * MASKS * BATCH * F_IN * U_OUT
+BYTES = MASKS * BATCH * (2 * F_IN + 2 * U_OUT + 4 * U_OUT) + 4 * MASKS * F_IN * U_OUT
+
+
+def tile_paralleldense_v_kernel(tc, x, W, b, z, grad_out, out):
+    nc = tc.nc
+    x_rows = x.rearrange("(p j) m f -> p j m f", j=PACK)
+    z_rows = z.rearrange("(p j) m u -> p j m u", j=PACK)
+    g_rows = grad_out.rearrange("(p j) (m u) -> p j m u", j=PACK, m=MASKS)
+
+    with ExitStack() as ctx:
+        keep = ctx.enter_context(tc.tile_pool(name="keep", bufs=1))
+        z_pool = ctx.enter_context(tc.tile_pool(name="z_pool", bufs=MASKS // Z_MASKS))
+        psum = ctx.enter_context(tc.psum_pool(name="psum", bufs=8))
+
+        x_codes = keep.tile([P, MASKS, F_IN], U32, align_bytes=64)
+        x_scales = keep.tile([P, MASKS, F_IN], U8, align_bytes=64)
+        g_raw = keep.tile([P, PACK, MASKS, U_OUT], BF16)
+
+        with tc.tile_pool(name="x_stage", bufs=2) as x_stage:
+            x_raws = []
+            for h in range(MASKS // X_MASKS):
+                x_raw = x_stage.tile([P, PACK, X_MASKS, F_IN], BF16)
+                nc.sync.dma_start(
+                    out=x_raw[:], in_=x_rows[:, :, h * X_MASKS : (h + 1) * X_MASKS, :]
+                )
+                x_raws.append(x_raw)
+            for j in range(0, PACK, 2):
+                nc.sync.dma_start(out=g_raw[:, j : j + 2], in_=g_rows[:, j : j + 2])
+            z_raws = []
+            for c in range(MASKS // Z_MASKS):
+                z_raw = z_pool.tile([P, PACK, Z_MASKS, U_OUT], F32)
+                nc.sync.dma_start(
+                    out=z_raw[:], in_=z_rows[:, :, c * Z_MASKS : (c + 1) * Z_MASKS, :]
+                )
+                z_raws.append(z_raw)
+
+            x_grouped = []
+            for m in range(MASKS + 1):
+                if m < MASKS:
+                    x_grp = x_stage.tile([P, F_IN, PACK], BF16, align_bytes=64)
+                    nc.vector.tensor_copy(
+                        out=x_grp[:].rearrange("p (c i) j -> p c j i", i=4),
+                        in_=x_raws[m // X_MASKS][:, :, m % X_MASKS, :].rearrange(
+                            "p j (c i) -> p c j i", i=4
+                        ),
+                    )
+                    x_grouped.append(x_grp)
+                if m > 0:
+                    nc.vector.quantize_mx(
+                        out=x_codes[:, m - 1, :].bitcast(E4M3_X4),
+                        scales=x_scales[:, m - 1, :],
+                        in_=x_grouped[m - 1][:].rearrange("p f j -> p (f j)"),
+                    )
+
+        dz_stage = ctx.enter_context(tc.tile_pool(name="dz_stage", bufs=2))
+        results = ctx.enter_context(tc.tile_pool(name="results", bufs=MASKS))
+
+        dz_grouped = []
+        for m in range(MASKS + 1):
+            if m < MASKS:
+                dz_grp = dz_stage.tile([P, U_OUT, PACK], BF16, align_bytes=64)
+                nc.vector.scalar_tensor_tensor(
+                    out=dz_grp[:],
+                    in0=z_raws[m // Z_MASKS][:, :, m % Z_MASKS, :].rearrange("p j u -> p u j"),
+                    scalar=0.0,
+                    in1=g_raw[:, :, m, :].rearrange("p j u -> p u j"),
+                    op0=ALU.is_gt,
+                    op1=ALU.mult,
+                )
+                dz_grouped.append(dz_grp)
+            if m > 0:
+                done = m - 1
+                dz_codes = dz_stage.tile([P, U_OUT], U32, align_bytes=64)
+                dz_scales = dz_stage.tile([P, U_OUT], U8, align_bytes=64)
+                nc.vector.quantize_mx(
+                    out=dz_codes[:].bitcast(E5M2_X4),
+                    scales=dz_scales[:],
+                    in_=dz_grouped[done][:].rearrange("p u j -> p (u j)"),
+                )
+                result = results.tile([P, F_TILES, U_OUT], F32)
+                for t in range(F_TILES):
+                    f_cols = slice(t * P, (t + 1) * P)
+                    acc = psum.tile([P, U_OUT], F32)
+                    nc.tensor.matmul_mx(
+                        out=acc[:],
+                        lhsT=x_codes[:, done, f_cols].bitcast(E4M3_X4),
+                        lhsT_scale=x_scales[:, done, f_cols],
+                        rhs=dz_codes[:].bitcast(E5M2_X4),
+                        rhs_scale=dz_scales[:],
+                        start=True,
+                        stop=True,
+                    )
+                    nc.scalar.copy(out=result[:, t, :], in_=acc[:])
+                nc.sync.dma_start(
+                    out=out[done].rearrange("(t p) u -> p t u", p=P), in_=result[:]
+                )

@@ -30,12 +30,12 @@ def tile_paralleldense_v_kernel(tc, x, W, b, z, grad_out, out):
 
     with ExitStack() as ctx:
         keep = ctx.enter_context(tc.tile_pool(name="keep", bufs=1))
+        g_pool = ctx.enter_context(tc.tile_pool(name="g_pool", bufs=MASKS // X_MASKS))
         z_pool = ctx.enter_context(tc.tile_pool(name="z_pool", bufs=MASKS // Z_MASKS))
         psum = ctx.enter_context(tc.psum_pool(name="psum", bufs=8))
 
         x_codes = keep.tile([P, MASKS, F_IN], U32, align_bytes=64)
         x_scales = keep.tile([P, MASKS, F_IN], U8, align_bytes=64)
-        g_raw = keep.tile([P, PACK, MASKS, U_OUT], BF16)
 
         with tc.tile_pool(name="x_stage", bufs=2) as x_stage:
             x_raws = []
@@ -45,24 +45,27 @@ def tile_paralleldense_v_kernel(tc, x, W, b, z, grad_out, out):
                     out=x_raw[:], in_=x_rows[:, :, h * X_MASKS : (h + 1) * X_MASKS, :]
                 )
                 x_raws.append(x_raw)
-            for j in range(0, PACK, 2):
-                nc.sync.dma_start(out=g_raw[:, j : j + 2], in_=g_rows[:, j : j + 2])
+            g_raws = []
             z_raws = []
-            for c in range(MASKS // Z_MASKS):
-                z_raw = z_pool.tile([P, PACK, Z_MASKS, U_OUT], F32)
+            for h in range(MASKS // X_MASKS):
+                g_raw = g_pool.tile([P, PACK, X_MASKS, U_OUT], BF16)
                 nc.sync.dma_start(
-                    out=z_raw[:], in_=z_rows[:, :, c * Z_MASKS : (c + 1) * Z_MASKS, :]
+                    out=g_raw[:], in_=g_rows[:, :, h * X_MASKS : (h + 1) * X_MASKS, :]
                 )
-                z_raws.append(z_raw)
+                g_raws.append(g_raw)
+                for first in range(h * X_MASKS, (h + 1) * X_MASKS, Z_MASKS):
+                    z_raw = z_pool.tile([P, PACK, Z_MASKS, U_OUT], F32)
+                    nc.sync.dma_start(out=z_raw[:], in_=z_rows[:, :, first : first + Z_MASKS, :])
+                    z_raws.append(z_raw)
 
             x_grouped = []
             for m in range(MASKS + 1):
                 if m < MASKS:
-                    x_grp = x_stage.tile([P, F_IN, PACK], BF16, align_bytes=64)
+                    x_grp = x_stage.tile([P, F_TILES, P, PACK], BF16, align_bytes=64)
                     nc.vector.tensor_copy(
-                        out=x_grp[:].rearrange("p (c i) j -> p c j i", i=4),
+                        out=x_grp[:].rearrange("p t c j -> p c j t"),
                         in_=x_raws[m // X_MASKS][:, :, m % X_MASKS, :].rearrange(
-                            "p j (c i) -> p c j i", i=4
+                            "p j (c t) -> p c j t", t=F_TILES
                         ),
                     )
                     x_grouped.append(x_grp)
@@ -70,7 +73,7 @@ def tile_paralleldense_v_kernel(tc, x, W, b, z, grad_out, out):
                     nc.vector.quantize_mx(
                         out=x_codes[:, m - 1, :].bitcast(E4M3_X4),
                         scales=x_scales[:, m - 1, :],
-                        in_=x_grouped[m - 1][:].rearrange("p f j -> p (f j)"),
+                        in_=x_grouped[m - 1][:].rearrange("p t c j -> p (t c j)"),
                     )
 
         dz_stage = ctx.enter_context(tc.tile_pool(name="dz_stage", bufs=2))
@@ -84,7 +87,7 @@ def tile_paralleldense_v_kernel(tc, x, W, b, z, grad_out, out):
                     out=dz_grp[:],
                     in0=z_raws[m // Z_MASKS][:, :, m % Z_MASKS, :].rearrange("p j u -> p u j"),
                     scalar=0.0,
-                    in1=g_raw[:, :, m, :].rearrange("p j u -> p u j"),
+                    in1=g_raws[m // X_MASKS][:, :, m % X_MASKS, :].rearrange("p j u -> p u j"),
                     op0=ALU.is_gt,
                     op1=ALU.mult,
                 )
@@ -113,5 +116,5 @@ def tile_paralleldense_v_kernel(tc, x, W, b, z, grad_out, out):
                     )
                     nc.scalar.copy(out=result[:, t, :], in_=acc[:])
                 nc.sync.dma_start(
-                    out=out[done].rearrange("(t p) u -> p t u", p=P), in_=result[:]
+                    out=out[done].rearrange("(c t) u -> c t u", t=F_TILES), in_=result[:]
                 )

@@ -61,11 +61,11 @@ def tile_paralleldense_v_kernel(tc, x, W, b, z, grad_out, out):
             x_grouped = []
             for m in range(MASKS + 1):
                 if m < MASKS:
-                    x_grp = x_stage.tile([P, F_TILES, P, PACK], BF16, align_bytes=64)
+                    x_grp = x_stage.tile([P, F_IN, PACK], BF16, align_bytes=64)
                     nc.vector.tensor_copy(
-                        out=x_grp[:].rearrange("p t c j -> p c j t"),
+                        out=x_grp[:].rearrange("p (c i) j -> p c j i", i=4),
                         in_=x_raws[m // X_MASKS][:, :, m % X_MASKS, :].rearrange(
-                            "p j (c t) -> p c j t", t=F_TILES
+                            "p j (c i) -> p c j i", i=4
                         ),
                     )
                     x_grouped.append(x_grp)
@@ -73,7 +73,7 @@ def tile_paralleldense_v_kernel(tc, x, W, b, z, grad_out, out):
                     nc.vector.quantize_mx(
                         out=x_codes[:, m - 1, :].bitcast(E4M3_X4),
                         scales=x_scales[:, m - 1, :],
-                        in_=x_grouped[m - 1][:].rearrange("p t c j -> p (t c j)"),
+                        in_=x_grouped[m - 1][:].rearrange("p f j -> p (f j)"),
                     )
 
         dz_stage = ctx.enter_context(tc.tile_pool(name="dz_stage", bufs=2))
@@ -116,5 +116,5 @@ def tile_paralleldense_v_kernel(tc, x, W, b, z, grad_out, out):
                     )
                     nc.scalar.copy(out=result[:, t, :], in_=acc[:])
                 nc.sync.dma_start(
-                    out=out[done].rearrange("(c t) u -> c t u", t=F_TILES), in_=result[:]
+                    out=out[done].rearrange("(t p) u -> p t u", p=P), in_=result[:]
                 )

@@ -17,6 +17,7 @@ assert BATCH == P * PACK
 F_TILES = F_IN // P
 X_MASKS = 4
 Z_MASKS = 2
+STORE_TILES = 2
 
 FLOPS = 2 * MASKS * BATCH * F_IN * U_OUT
 BYTES = MASKS * BATCH * (2 * F_IN + 2 * U_OUT + 4 * U_OUT) + 4 * MASKS * F_IN * U_OUT
@@ -61,11 +62,11 @@ def tile_paralleldense_v_kernel(tc, x, W, b, z, grad_out, out):
             x_grouped = []
             for m in range(MASKS + 1):
                 if m < MASKS:
-                    x_grp = x_stage.tile([P, F_IN, PACK], BF16, align_bytes=64)
+                    x_grp = x_stage.tile([P, F_TILES, P, PACK], BF16, align_bytes=64)
                     nc.vector.tensor_copy(
-                        out=x_grp[:].rearrange("p (c i) j -> p c j i", i=4),
+                        out=x_grp[:].rearrange("p t c j -> p c j t"),
                         in_=x_raws[m // X_MASKS][:, :, m % X_MASKS, :].rearrange(
-                            "p j (c i) -> p c j i", i=4
+                            "p j (c t) -> p c j t", t=F_TILES
                         ),
                     )
                     x_grouped.append(x_grp)
@@ -73,7 +74,7 @@ def tile_paralleldense_v_kernel(tc, x, W, b, z, grad_out, out):
                     nc.vector.quantize_mx(
                         out=x_codes[:, m - 1, :].bitcast(E4M3_X4),
                         scales=x_scales[:, m - 1, :],
-                        in_=x_grouped[m - 1][:].rearrange("p f j -> p (f j)"),
+                        in_=x_grouped[m - 1][:].rearrange("p t c j -> p (t c j)"),
                     )
 
         dz_stage = ctx.enter_context(tc.tile_pool(name="dz_stage", bufs=2))
@@ -102,6 +103,7 @@ def tile_paralleldense_v_kernel(tc, x, W, b, z, grad_out, out):
                     in_=dz_grouped[done][:].rearrange("p u j -> p (u j)"),
                 )
                 result = results.tile([P, F_TILES, U_OUT], F32)
+                out_rows = out[done].rearrange("(c t) u -> c t u", t=F_TILES)
                 for t in range(F_TILES):
                     f_cols = slice(t * P, (t + 1) * P)
                     acc = psum.tile([P, U_OUT], F32)
@@ -114,7 +116,10 @@ def tile_paralleldense_v_kernel(tc, x, W, b, z, grad_out, out):
                         start=True,
                         stop=True,
                     )
-                    nc.scalar.copy(out=result[:, t, :], in_=acc[:])
-                nc.sync.dma_start(
-                    out=out[done].rearrange("(t p) u -> p t u", p=P), in_=result[:]
-                )
+                    if m < MASKS:
+                        nc.scalar.copy(out=result[:, t, :], in_=acc[:])
+                    else:
+                        nc.vector.tensor_copy(out=result[:, t, :], in_=acc[:])
+                    if (t + 1) % STORE_TILES == 0:
+                        tiles = slice(t + 1 - STORE_TILES, t + 1)
+                        nc.sync.dma_start(out=out_rows[:, tiles, :], in_=result[:, tiles, :])

@@ -15,9 +15,10 @@ PACK = 4
 BATCH, MASKS, F_IN, U_OUT = 512, 8, 512, 512
 assert BATCH == P * PACK
 F_TILES = F_IN // P
-X_MASKS = 4
-Z_MASKS = 2
+GROUP = 2
+GROUPS = MASKS // GROUP
 STORE_TILES = 2
+RESULT_BUFS = 6
 
 FLOPS = 2 * MASKS * BATCH * F_IN * U_OUT
 BYTES = MASKS * BATCH * (2 * F_IN + 2 * U_OUT + 4 * U_OUT) + 4 * MASKS * F_IN * U_OUT
@@ -31,92 +32,79 @@ def tile_paralleldense_v_kernel(tc, x, W, b, z, grad_out, out):
 
     with ExitStack() as ctx:
         keep = ctx.enter_context(tc.tile_pool(name="keep", bufs=1))
-        g_pool = ctx.enter_context(tc.tile_pool(name="g_pool", bufs=MASKS // X_MASKS))
-        z_pool = ctx.enter_context(tc.tile_pool(name="z_pool", bufs=MASKS // Z_MASKS))
+        raw = ctx.enter_context(tc.tile_pool(name="raw", bufs=GROUPS))
+        stage = ctx.enter_context(tc.tile_pool(name="stage", bufs=3))
+        results = ctx.enter_context(tc.tile_pool(name="results", bufs=RESULT_BUFS))
         psum = ctx.enter_context(tc.psum_pool(name="psum", bufs=8))
 
         x_codes = keep.tile([P, MASKS, F_IN], U32, align_bytes=64)
         x_scales = keep.tile([P, MASKS, F_IN], U8, align_bytes=64)
 
-        with tc.tile_pool(name="x_stage", bufs=2) as x_stage:
-            x_raws = []
-            for h in range(MASKS // X_MASKS):
-                x_raw = x_stage.tile([P, PACK, X_MASKS, F_IN], BF16)
-                nc.sync.dma_start(
-                    out=x_raw[:], in_=x_rows[:, :, h * X_MASKS : (h + 1) * X_MASKS, :]
-                )
-                x_raws.append(x_raw)
-            g_raws = []
-            z_raws = []
-            for h in range(MASKS // X_MASKS):
-                g_raw = g_pool.tile([P, PACK, X_MASKS, U_OUT], BF16)
-                nc.sync.dma_start(
-                    out=g_raw[:], in_=g_rows[:, :, h * X_MASKS : (h + 1) * X_MASKS, :]
-                )
-                g_raws.append(g_raw)
-                for first in range(h * X_MASKS, (h + 1) * X_MASKS, Z_MASKS):
-                    z_raw = z_pool.tile([P, PACK, Z_MASKS, U_OUT], F32)
-                    nc.sync.dma_start(out=z_raw[:], in_=z_rows[:, :, first : first + Z_MASKS, :])
-                    z_raws.append(z_raw)
+        g_raws = []
+        z_raws = []
+        x_raws = []
+        for h in range(GROUPS):
+            pair = slice(h * GROUP, (h + 1) * GROUP)
+            g_raw = raw.tile([P, PACK, GROUP, U_OUT], BF16)
+            nc.sync.dma_start(out=g_raw[:], in_=g_rows[:, :, pair, :])
+            g_raws.append(g_raw)
+            z_raw = raw.tile([P, PACK, GROUP, U_OUT], F32)
+            nc.sync.dma_start(out=z_raw[:], in_=z_rows[:, :, pair, :])
+            z_raws.append(z_raw)
+            x_raw = raw.tile([P, PACK, GROUP, F_IN], BF16)
+            nc.sync.dma_start(out=x_raw[:], in_=x_rows[:, :, pair, :])
+            x_raws.append(x_raw)
 
-            x_grouped = []
-            for m in range(MASKS + 1):
-                if m < MASKS:
-                    x_grp = x_stage.tile([P, F_TILES, P, PACK], BF16, align_bytes=64)
-                    nc.vector.tensor_copy(
-                        out=x_grp[:].rearrange("p t c j -> p c j t"),
-                        in_=x_raws[m // X_MASKS][:, :, m % X_MASKS, :].rearrange(
-                            "p j (c t) -> p c j t", t=F_TILES
-                        ),
-                    )
-                    x_grouped.append(x_grp)
-                if m > 0:
-                    nc.vector.quantize_mx(
-                        out=x_codes[:, m - 1, :].bitcast(E4M3_X4),
-                        scales=x_scales[:, m - 1, :],
-                        in_=x_grouped[m - 1][:].rearrange("p t c j -> p (t c j)"),
-                    )
-
-        dz_stage = ctx.enter_context(tc.tile_pool(name="dz_stage", bufs=2))
-        results = ctx.enter_context(tc.tile_pool(name="results", bufs=MASKS))
-
-        dz_grouped = []
-        for m in range(MASKS + 1):
-            if m < MASKS:
-                dz_grp = dz_stage.tile([P, U_OUT, PACK], BF16, align_bytes=64)
+        for h in range(GROUPS):
+            group = range(h * GROUP, (h + 1) * GROUP)
+            dz_grouped = {}
+            x_grouped = {}
+            for m in group:
+                dz_grp = stage.tile([P, U_OUT, PACK], BF16, align_bytes=64)
                 nc.vector.scalar_tensor_tensor(
                     out=dz_grp[:],
-                    in0=z_raws[m // Z_MASKS][:, :, m % Z_MASKS, :].rearrange("p j u -> p u j"),
+                    in0=z_raws[h][:, :, m % GROUP, :].rearrange("p j u -> p u j"),
                     scalar=0.0,
-                    in1=g_raws[m // X_MASKS][:, :, m % X_MASKS, :].rearrange("p j u -> p u j"),
+                    in1=g_raws[h][:, :, m % GROUP, :].rearrange("p j u -> p u j"),
                     op0=ALU.is_gt,
                     op1=ALU.mult,
                 )
-                dz_grouped.append(dz_grp)
-            if m > 0:
-                done = m - 1
-                dz_codes = dz_stage.tile([P, U_OUT], U32, align_bytes=64)
-                dz_scales = dz_stage.tile([P, U_OUT], U8, align_bytes=64)
+                dz_grouped[m] = dz_grp
+            for m in group:
+                x_grp = stage.tile([P, F_TILES, P, PACK], BF16, align_bytes=64)
+                nc.scalar.copy(
+                    out=x_grp[:].rearrange("p t c j -> p c j t"),
+                    in_=x_raws[h][:, :, m % GROUP, :].rearrange("p j (c t) -> p c j t", t=F_TILES),
+                )
+                x_grouped[m] = x_grp
+            for m in group:
+                dz_codes = stage.tile([P, U_OUT], U32, align_bytes=64)
+                dz_scales = stage.tile([P, U_OUT], U8, align_bytes=64)
                 nc.vector.quantize_mx(
                     out=dz_codes[:].bitcast(E5M2_X4),
                     scales=dz_scales[:],
-                    in_=dz_grouped[done][:].rearrange("p u j -> p (u j)"),
+                    in_=dz_grouped[m][:].rearrange("p u j -> p (u j)"),
+                )
+                nc.vector.quantize_mx(
+                    out=x_codes[:, m, :].bitcast(E4M3_X4),
+                    scales=x_scales[:, m, :],
+                    in_=x_grouped[m][:].rearrange("p t c j -> p (t c j)"),
                 )
                 result = results.tile([P, F_TILES, U_OUT], F32)
-                out_rows = out[done].rearrange("(c t) u -> c t u", t=F_TILES)
+                out_rows = out[m].rearrange("(c t) u -> c t u", t=F_TILES)
                 for t in range(F_TILES):
                     f_cols = slice(t * P, (t + 1) * P)
                     acc = psum.tile([P, U_OUT], F32)
                     nc.tensor.matmul_mx(
                         out=acc[:],
-                        lhsT=x_codes[:, done, f_cols].bitcast(E4M3_X4),
-                        lhsT_scale=x_scales[:, done, f_cols],
+                        lhsT=x_codes[:, m, f_cols].bitcast(E4M3_X4),
+                        lhsT_scale=x_scales[:, m, f_cols],
                         rhs=dz_codes[:].bitcast(E5M2_X4),
                         rhs_scale=dz_scales[:],
                         start=True,
                         stop=True,
                     )
-                    if m < MASKS:
+                    if m < MASKS - 1:
                         nc.scalar.copy(out=result[:, t, :], in_=acc[:])
                     else:
                         nc.vector.tensor_copy(out=result[:, t, :], in_=acc[:])

@@ -17,8 +17,7 @@ assert BATCH == P * PACK
 F_TILES = F_IN // P
 GROUP = 2
 GROUPS = MASKS // GROUP
-STORE_TILES = 2
-RESULT_BUFS = 6
+STORES = ((0, 4, 0, 4), (4, 2, 0, 4), (6, 1, 0, 4), (7, 1, 0, 2), (7, 1, 2, 2))
 
 FLOPS = 2 * MASKS * BATCH * F_IN * U_OUT
 BYTES = MASKS * BATCH * (2 * F_IN + 2 * U_OUT + 4 * U_OUT) + 4 * MASKS * F_IN * U_OUT
@@ -33,12 +32,14 @@ def tile_paralleldense_v_kernel(tc, x, W, b, z, grad_out, out):
     with ExitStack() as ctx:
         keep = ctx.enter_context(tc.tile_pool(name="keep", bufs=1))
         raw = ctx.enter_context(tc.tile_pool(name="raw", bufs=GROUPS))
+        z_pool = ctx.enter_context(tc.tile_pool(name="z_pool", bufs=GROUPS - 1))
         stage = ctx.enter_context(tc.tile_pool(name="stage", bufs=3))
-        results = ctx.enter_context(tc.tile_pool(name="results", bufs=RESULT_BUFS))
         psum = ctx.enter_context(tc.psum_pool(name="psum", bufs=8))
 
         x_codes = keep.tile([P, MASKS, F_IN], U32, align_bytes=64)
         x_scales = keep.tile([P, MASKS, F_IN], U8, align_bytes=64)
+        result = keep.tile([P, MASKS, F_TILES, U_OUT], F32)
+        out_rows = out.rearrange("m (c t) u -> c m t u", t=F_TILES)
 
         g_raws = []
         z_raws = []
@@ -48,7 +49,7 @@ def tile_paralleldense_v_kernel(tc, x, W, b, z, grad_out, out):
             g_raw = raw.tile([P, PACK, GROUP, U_OUT], BF16)
             nc.sync.dma_start(out=g_raw[:], in_=g_rows[:, :, pair, :])
             g_raws.append(g_raw)
-            z_raw = raw.tile([P, PACK, GROUP, U_OUT], F32)
+            z_raw = z_pool.tile([P, PACK, GROUP, U_OUT], F32)
             nc.sync.dma_start(out=z_raw[:], in_=z_rows[:, :, pair, :])
             z_raws.append(z_raw)
             x_raw = raw.tile([P, PACK, GROUP, F_IN], BF16)
@@ -90,8 +91,6 @@ def tile_paralleldense_v_kernel(tc, x, W, b, z, grad_out, out):
                     scales=x_scales[:, m, :],
                     in_=x_grouped[m][:].rearrange("p t c j -> p (t c j)"),
                 )
-                result = results.tile([P, F_TILES, U_OUT], F32)
-                out_rows = out[m].rearrange("(c t) u -> c t u", t=F_TILES)
                 for t in range(F_TILES):
                     f_cols = slice(t * P, (t + 1) * P)
                     acc = psum.tile([P, U_OUT], F32)
@@ -105,9 +104,12 @@ def tile_paralleldense_v_kernel(tc, x, W, b, z, grad_out, out):
                         stop=True,
                     )
                     if m < MASKS - 1:
-                        nc.scalar.copy(out=result[:, t, :], in_=acc[:])
+                        nc.scalar.copy(out=result[:, m, t, :], in_=acc[:])
                     else:
-                        nc.vector.tensor_copy(out=result[:, t, :], in_=acc[:])
-                    if (t + 1) % STORE_TILES == 0:
-                        tiles = slice(t + 1 - STORE_TILES, t + 1)
-                        nc.sync.dma_start(out=out_rows[:, tiles, :], in_=result[:, tiles, :])
+                        nc.vector.tensor_copy(out=result[:, m, t, :], in_=acc[:])
+                    for m0, n_m, t0, n_t in STORES:
+                        if (m, t) == (m0 + n_m - 1, t0 + n_t - 1):
+                            nc.sync.dma_start(
+                                out=out_rows[:, m0 : m0 + n_m, t0 : t0 + n_t, :],
+                                in_=result[:, m0 : m0 + n_m, t0 : t0 + n_t, :],
+                            )

@@ -17,7 +17,9 @@ assert BATCH == P * PACK
 F_TILES = F_IN // P
 GROUP = 2
 GROUPS = MASKS // GROUP
-STORES = ((0, 4, 0, 4), (4, 2, 0, 4), (6, 1, 0, 4), (7, 1, 0, 2), (7, 1, 2, 2))
+STORES = ((0, 2, 0, 4), (2, 2, 0, 4), (4, 2, 0, 4), (6, 1, 0, 4), (7, 1, 0, 2), (7, 1, 2, 2))
+X_ON_VECTOR = 2
+X_EARLY = 4
 
 FLOPS = 2 * MASKS * BATCH * F_IN * U_OUT
 BYTES = MASKS * BATCH * (2 * F_IN + 2 * U_OUT + 4 * U_OUT) + 4 * MASKS * F_IN * U_OUT
@@ -28,88 +30,113 @@ def tile_paralleldense_v_kernel(tc, x, W, b, z, grad_out, out):
     x_rows = x.rearrange("(p j) m f -> p j m f", j=PACK)
     z_rows = z.rearrange("(p j) m u -> p j m u", j=PACK)
     g_rows = grad_out.rearrange("(p j) (m u) -> p j m u", j=PACK, m=MASKS)
+    out_rows = out.rearrange("m (c t) u -> c m t u", t=F_TILES)
 
     with ExitStack() as ctx:
         keep = ctx.enter_context(tc.tile_pool(name="keep", bufs=1))
-        raw = ctx.enter_context(tc.tile_pool(name="raw", bufs=GROUPS))
+        g_pool = ctx.enter_context(tc.tile_pool(name="g_pool", bufs=GROUPS))
         z_pool = ctx.enter_context(tc.tile_pool(name="z_pool", bufs=GROUPS - 1))
-        stage = ctx.enter_context(tc.tile_pool(name="stage", bufs=3))
+        x_stage = ctx.enter_context(tc.tile_pool(name="x_stage", bufs=4))
+        dz_stage = ctx.enter_context(tc.tile_pool(name="dz_stage", bufs=3))
         psum = ctx.enter_context(tc.psum_pool(name="psum", bufs=8))
 
+        x_raw = keep.tile([P, PACK, MASKS, F_IN], BF16)
         x_codes = keep.tile([P, MASKS, F_IN], U32, align_bytes=64)
         x_scales = keep.tile([P, MASKS, F_IN], U8, align_bytes=64)
         result = keep.tile([P, MASKS, F_TILES, U_OUT], F32)
-        out_rows = out.rearrange("m (c t) u -> c m t u", t=F_TILES)
 
+        nc.sync.dma_start(out=x_raw[:], in_=x_rows)
         g_raws = []
         z_raws = []
-        x_raws = []
         for h in range(GROUPS):
             pair = slice(h * GROUP, (h + 1) * GROUP)
-            g_raw = raw.tile([P, PACK, GROUP, U_OUT], BF16)
+            g_raw = g_pool.tile([P, PACK, GROUP, U_OUT], BF16)
             nc.sync.dma_start(out=g_raw[:], in_=g_rows[:, :, pair, :])
             g_raws.append(g_raw)
             z_raw = z_pool.tile([P, PACK, GROUP, U_OUT], F32)
             nc.sync.dma_start(out=z_raw[:], in_=z_rows[:, :, pair, :])
             z_raws.append(z_raw)
-            x_raw = raw.tile([P, PACK, GROUP, F_IN], BF16)
-            nc.sync.dma_start(out=x_raw[:], in_=x_rows[:, :, pair, :])
-            x_raws.append(x_raw)
 
-        for h in range(GROUPS):
-            group = range(h * GROUP, (h + 1) * GROUP)
-            dz_grouped = {}
-            x_grouped = {}
-            for m in group:
-                dz_grp = stage.tile([P, U_OUT, PACK], BF16, align_bytes=64)
-                nc.vector.scalar_tensor_tensor(
-                    out=dz_grp[:],
-                    in0=z_raws[h][:, :, m % GROUP, :].rearrange("p j u -> p u j"),
-                    scalar=0.0,
-                    in1=g_raws[h][:, :, m % GROUP, :].rearrange("p j u -> p u j"),
-                    op0=ALU.is_gt,
-                    op1=ALU.mult,
+        x_grouped = {}
+        dz_grouped = {}
+        dz_quantised = {}
+
+        def group_x(m):
+            x_grp = x_stage.tile([P, F_TILES, P, PACK], BF16, align_bytes=64)
+            dst = x_grp[:].rearrange("p t c j -> p c j t")
+            src = x_raw[:, :, m, :].rearrange("p j (c t) -> p c j t", t=F_TILES)
+            if m < X_ON_VECTOR:
+                nc.vector.tensor_copy(out=dst, in_=src)
+            else:
+                nc.scalar.copy(out=dst, in_=src)
+            x_grouped[m] = x_grp
+
+        def quantise_x(m):
+            nc.vector.quantize_mx(
+                out=x_codes[:, m, :].bitcast(E4M3_X4),
+                scales=x_scales[:, m, :],
+                in_=x_grouped[m][:].rearrange("p t c j -> p (t c j)"),
+            )
+
+        def mask_dz(m):
+            dz_grp = dz_stage.tile([P, U_OUT, PACK], BF16, align_bytes=64)
+            nc.vector.scalar_tensor_tensor(
+                out=dz_grp[:],
+                in0=z_raws[m // GROUP][:, :, m % GROUP, :].rearrange("p j u -> p u j"),
+                scalar=0.0,
+                in1=g_raws[m // GROUP][:, :, m % GROUP, :].rearrange("p j u -> p u j"),
+                op0=ALU.is_gt,
+                op1=ALU.mult,
+            )
+            dz_grouped[m] = dz_grp
+
+        def quantise_dz(m):
+            dz_codes = dz_stage.tile([P, U_OUT], U32, align_bytes=64)
+            dz_scales = dz_stage.tile([P, U_OUT], U8, align_bytes=64)
+            nc.vector.quantize_mx(
+                out=dz_codes[:].bitcast(E5M2_X4),
+                scales=dz_scales[:],
+                in_=dz_grouped[m][:].rearrange("p u j -> p (u j)"),
+            )
+            dz_quantised[m] = (dz_codes, dz_scales)
+
+        def multiply_and_store(m):
+            dz_codes, dz_scales = dz_quantised[m]
+            for t in range(F_TILES):
+                f_cols = slice(t * P, (t + 1) * P)
+                acc = psum.tile([P, U_OUT], F32)
+                nc.tensor.matmul_mx(
+                    out=acc[:],
+                    lhsT=x_codes[:, m, f_cols].bitcast(E4M3_X4),
+                    lhsT_scale=x_scales[:, m, f_cols],
+                    rhs=dz_codes[:].bitcast(E5M2_X4),
+                    rhs_scale=dz_scales[:],
+                    start=True,
+                    stop=True,
                 )
-                dz_grouped[m] = dz_grp
-            for m in group:
-                x_grp = stage.tile([P, F_TILES, P, PACK], BF16, align_bytes=64)
-                nc.scalar.copy(
-                    out=x_grp[:].rearrange("p t c j -> p c j t"),
-                    in_=x_raws[h][:, :, m % GROUP, :].rearrange("p j (c t) -> p c j t", t=F_TILES),
-                )
-                x_grouped[m] = x_grp
-            for m in group:
-                dz_codes = stage.tile([P, U_OUT], U32, align_bytes=64)
-                dz_scales = stage.tile([P, U_OUT], U8, align_bytes=64)
-                nc.vector.quantize_mx(
-                    out=dz_codes[:].bitcast(E5M2_X4),
-                    scales=dz_scales[:],
-                    in_=dz_grouped[m][:].rearrange("p u j -> p (u j)"),
-                )
-                nc.vector.quantize_mx(
-                    out=x_codes[:, m, :].bitcast(E4M3_X4),
-                    scales=x_scales[:, m, :],
-                    in_=x_grouped[m][:].rearrange("p t c j -> p (t c j)"),
-                )
-                for t in range(F_TILES):
-                    f_cols = slice(t * P, (t + 1) * P)
-                    acc = psum.tile([P, U_OUT], F32)
-                    nc.tensor.matmul_mx(
-                        out=acc[:],
-                        lhsT=x_codes[:, m, f_cols].bitcast(E4M3_X4),
-                        lhsT_scale=x_scales[:, m, f_cols],
-                        rhs=dz_codes[:].bitcast(E5M2_X4),
-                        rhs_scale=dz_scales[:],
-                        start=True,
-                        stop=True,
-                    )
-                    if m < MASKS - 1:
-                        nc.scalar.copy(out=result[:, m, t, :], in_=acc[:])
-                    else:
-                        nc.vector.tensor_copy(out=result[:, m, t, :], in_=acc[:])
-                    for m0, n_m, t0, n_t in STORES:
-                        if (m, t) == (m0 + n_m - 1, t0 + n_t - 1):
-                            nc.sync.dma_start(
-                                out=out_rows[:, m0 : m0 + n_m, t0 : t0 + n_t, :],
-                                in_=result[:, m0 : m0 + n_m, t0 : t0 + n_t, :],
-                            )
+                if m == MASKS - 1 and t % 2 == 0:
+                    nc.vector.tensor_copy(out=result[:, m, t, :], in_=acc[:])
+                else:
+                    nc.scalar.copy(out=result[:, m, t, :], in_=acc[:])
+                for m0, n_m, t0, n_t in STORES:
+                    if (m, t) == (m0 + n_m - 1, t0 + n_t - 1):
+                        nc.sync.dma_start(
+                            out=out_rows[:, m0 : m0 + n_m, t0 : t0 + n_t, :],
+                            in_=result[:, m0 : m0 + n_m, t0 : t0 + n_t, :],
+                        )
+
+        for m in range(MASKS):
+            group_x(m)
+        for m in range(X_EARLY):
+            quantise_x(m)
+        for first in range(0, X_EARLY, GROUP):
+            for m in range(first, first + GROUP):
+                mask_dz(m)
+            for m in range(first, first + GROUP):
+                quantise_dz(m)
+                multiply_and_store(m)
+        for m in range(X_EARLY, MASKS):
+            mask_dz(m)
+            quantise_x(m)
+            quantise_dz(m)
+            multiply_and_store(m)

@@ -17,9 +17,8 @@ assert BATCH == P * PACK
 F_TILES = F_IN // P
 GROUP = 2
 GROUPS = MASKS // GROUP
-STORES = ((0, 2, 0, 4), (2, 2, 0, 4), (4, 2, 0, 4), (6, 1, 0, 4), (7, 1, 0, 2), (7, 1, 2, 2))
-X_ON_VECTOR = 2
-X_EARLY = 4
+STORES = ((0, 2, 0, 4), (2, 2, 0, 4), (4, 1, 0, 4), (5, 1, 0, 4), (6, 1, 0, 4), (7, 1, 0, 2), (7, 1, 2, 2))
+X_ON_VECTOR = 3
 
 FLOPS = 2 * MASKS * BATCH * F_IN * U_OUT
 BYTES = MASKS * BATCH * (2 * F_IN + 2 * U_OUT + 4 * U_OUT) + 4 * MASKS * F_IN * U_OUT
@@ -45,7 +44,6 @@ def tile_paralleldense_v_kernel(tc, x, W, b, z, grad_out, out):
         x_scales = keep.tile([P, MASKS, F_IN], U8, align_bytes=64)
         result = keep.tile([P, MASKS, F_TILES, U_OUT], F32)
 
-        nc.sync.dma_start(out=x_raw[:], in_=x_rows)
         g_raws = []
         z_raws = []
         for h in range(GROUPS):
@@ -56,6 +54,8 @@ def tile_paralleldense_v_kernel(tc, x, W, b, z, grad_out, out):
             z_raw = z_pool.tile([P, PACK, GROUP, U_OUT], F32)
             nc.sync.dma_start(out=z_raw[:], in_=z_rows[:, :, pair, :])
             z_raws.append(z_raw)
+            if h == 0:
+                nc.sync.dma_start(out=x_raw[:], in_=x_rows)
 
         x_grouped = {}
         dz_grouped = {}
@@ -125,17 +125,39 @@ def tile_paralleldense_v_kernel(tc, x, W, b, z, grad_out, out):
                             in_=result[:, m0 : m0 + n_m, t0 : t0 + n_t, :],
                         )
 
-        for m in range(MASKS):
-            group_x(m)
-        for m in range(X_EARLY):
-            quantise_x(m)
-        for first in range(0, X_EARLY, GROUP):
-            for m in range(first, first + GROUP):
-                mask_dz(m)
-            for m in range(first, first + GROUP):
-                quantise_dz(m)
-                multiply_and_store(m)
-        for m in range(X_EARLY, MASKS):
+        mask_dz(0)
+        mask_dz(1)
+        quantise_dz(0)
+        quantise_dz(1)
+        group_x(0)
+        group_x(3)
+        group_x(1)
+        group_x(4)
+        quantise_x(0)
+        group_x(2)
+        quantise_x(1)
+        quantise_x(3)
+        quantise_x(2)
+        quantise_x(4)
+        multiply_and_store(0)
+        multiply_and_store(1)
+        mask_dz(2)
+        mask_dz(3)
+        group_x(5)
+        group_x(6)
+        quantise_dz(2)
+        quantise_dz(3)
+        multiply_and_store(2)
+        multiply_and_store(3)
+        mask_dz(4)
+        mask_dz(5)
+        group_x(7)
+        quantise_dz(4)
+        multiply_and_store(4)
+        quantise_x(5)
+        quantise_dz(5)
+        multiply_and_store(5)
+        for m in (6, 7):
             mask_dz(m)
             quantise_x(m)
             quantise_dz(m)

@@ -125,40 +125,41 @@ def tile_paralleldense_v_kernel(tc, x, W, b, z, grad_out, out):
                             in_=result[:, m0 : m0 + n_m, t0 : t0 + n_t, :],
                         )
 
-        mask_dz(0)
-        mask_dz(1)
-        quantise_dz(0)
-        quantise_dz(1)
-        group_x(0)
-        group_x(3)
-        group_x(1)
-        group_x(4)
-        quantise_x(0)
-        group_x(2)
-        quantise_x(1)
-        quantise_x(3)
-        quantise_x(2)
-        quantise_x(4)
-        multiply_and_store(0)
-        multiply_and_store(1)
-        mask_dz(2)
-        mask_dz(3)
-        group_x(5)
-        group_x(6)
-        quantise_dz(2)
-        quantise_dz(3)
-        multiply_and_store(2)
-        multiply_and_store(3)
-        mask_dz(4)
-        mask_dz(5)
-        group_x(7)
-        quantise_dz(4)
-        multiply_and_store(4)
-        quantise_x(5)
-        quantise_dz(5)
-        multiply_and_store(5)
-        for m in (6, 7):
-            mask_dz(m)
-            quantise_x(m)
-            quantise_dz(m)
-            multiply_and_store(m)
+        with tc.manual_schedule():
+            mask_dz(0)
+            mask_dz(1)
+            quantise_dz(0)
+            quantise_dz(1)
+            group_x(0)
+            group_x(3)
+            group_x(1)
+            group_x(4)
+            quantise_x(0)
+            group_x(2)
+            quantise_x(1)
+            quantise_x(3)
+            quantise_x(2)
+            quantise_x(4)
+            multiply_and_store(0)
+            multiply_and_store(1)
+            mask_dz(2)
+            mask_dz(3)
+            group_x(5)
+            group_x(6)
+            quantise_dz(2)
+            quantise_dz(3)
+            multiply_and_store(2)
+            multiply_and_store(3)
+            mask_dz(4)
+            mask_dz(5)
+            group_x(7)
+            quantise_dz(4)
+            multiply_and_store(4)
+            quantise_x(5)
+            quantise_dz(5)
+            multiply_and_store(5)
+            for m in (6, 7):
+                mask_dz(m)
+                quantise_x(m)
+                quantise_dz(m)
+                multiply_and_store(m)

@@ -17,6 +17,7 @@ assert BATCH == P * PACK
 F_TILES = F_IN // P
 GROUP = 2
 GROUPS = MASKS // GROUP
+G_GROUP = 4
 STORES = ((0, 2, 0, 4), (2, 2, 0, 4), (4, 1, 0, 4), (5, 1, 0, 4), (6, 1, 0, 4), (7, 1, 0, 2), (7, 1, 2, 2))
 X_ON_VECTOR = 3
 
@@ -33,7 +34,7 @@ def tile_paralleldense_v_kernel(tc, x, W, b, z, grad_out, out):
 
     with ExitStack() as ctx:
         keep = ctx.enter_context(tc.tile_pool(name="keep", bufs=1))
-        g_pool = ctx.enter_context(tc.tile_pool(name="g_pool", bufs=GROUPS))
+        g_pool = ctx.enter_context(tc.tile_pool(name="g_pool", bufs=MASKS // G_GROUP))
         z_pool = ctx.enter_context(tc.tile_pool(name="z_pool", bufs=GROUPS - 1))
         x_stage = ctx.enter_context(tc.tile_pool(name="x_stage", bufs=4))
         dz_stage = ctx.enter_context(tc.tile_pool(name="dz_stage", bufs=3))
@@ -48,9 +49,12 @@ def tile_paralleldense_v_kernel(tc, x, W, b, z, grad_out, out):
         z_raws = []
         for h in range(GROUPS):
             pair = slice(h * GROUP, (h + 1) * GROUP)
-            g_raw = g_pool.tile([P, PACK, GROUP, U_OUT], BF16)
-            nc.sync.dma_start(out=g_raw[:], in_=g_rows[:, :, pair, :])
-            g_raws.append(g_raw)
+            if (h * GROUP) % G_GROUP == 0:
+                g_raw = g_pool.tile([P, PACK, G_GROUP, U_OUT], BF16)
+                nc.sync.dma_start(
+                    out=g_raw[:], in_=g_rows[:, :, h * GROUP : h * GROUP + G_GROUP, :]
+                )
+                g_raws.append(g_raw)
             z_raw = z_pool.tile([P, PACK, GROUP, U_OUT], F32)
             nc.sync.dma_start(out=z_raw[:], in_=z_rows[:, :, pair, :])
             z_raws.append(z_raw)
@@ -84,7 +88,7 @@ def tile_paralleldense_v_kernel(tc, x, W, b, z, grad_out, out):
                 out=dz_grp[:],
                 in0=z_raws[m // GROUP][:, :, m % GROUP, :].rearrange("p j u -> p u j"),
                 scalar=0.0,
-                in1=g_raws[m // GROUP][:, :, m % GROUP, :].rearrange("p j u -> p u j"),
+                in1=g_raws[m // G_GROUP][:, :, m % G_GROUP, :].rearrange("p j u -> p u j"),
                 op0=ALU.is_gt,
                 op1=ALU.mult,
             )

@@ -37,7 +37,8 @@ def tile_paralleldense_v_kernel(tc, x, W, b, z, grad_out, out):
         g_pool = ctx.enter_context(tc.tile_pool(name="g_pool", bufs=MASKS // G_GROUP))
         z_pool = ctx.enter_context(tc.tile_pool(name="z_pool", bufs=GROUPS - 1))
         x_stage = ctx.enter_context(tc.tile_pool(name="x_stage", bufs=4))
-        dz_stage = ctx.enter_context(tc.tile_pool(name="dz_stage", bufs=3))
+        dz_stage = ctx.enter_context(tc.tile_pool(name="dz_stage", bufs=2))
+        half_pool = ctx.enter_context(tc.tile_pool(name="half_pool", bufs=2))
         psum = ctx.enter_context(tc.psum_pool(name="psum", bufs=8))
 
         x_raw = keep.tile([P, PACK, MASKS, F_IN], BF16)
@@ -62,6 +63,7 @@ def tile_paralleldense_v_kernel(tc, x, W, b, z, grad_out, out):
                 nc.sync.dma_start(out=x_raw[:], in_=x_rows)
 
         x_grouped = {}
+        dz_halves = {}
         dz_grouped = {}
         dz_quantised = {}
 
@@ -83,14 +85,27 @@ def tile_paralleldense_v_kernel(tc, x, W, b, z, grad_out, out):
             )
 
         def mask_dz(m):
+            halves = half_pool.tile([P, PACK // 2, U_OUT, 2], BF16, align_bytes=64)
+            for r in range(PACK // 2):
+                rows = slice(2 * r, 2 * r + 2)
+                nc.vector.scalar_tensor_tensor(
+                    out=halves[:, r],
+                    in0=z_raws[m // GROUP][:, rows, m % GROUP, :].rearrange("p e u -> p u e"),
+                    scalar=0.0,
+                    in1=g_raws[m // G_GROUP][:, rows, m % G_GROUP, :].rearrange("p e u -> p u e"),
+                    op0=ALU.is_gt,
+                    op1=ALU.mult,
+                )
+            dz_halves[m] = halves
+
+        def interleave_dz(m):
             dz_grp = dz_stage.tile([P, U_OUT, PACK], BF16, align_bytes=64)
-            nc.vector.scalar_tensor_tensor(
-                out=dz_grp[:],
-                in0=z_raws[m // GROUP][:, :, m % GROUP, :].rearrange("p j u -> p u j"),
-                scalar=0.0,
-                in1=g_raws[m // G_GROUP][:, :, m % G_GROUP, :].rearrange("p j u -> p u j"),
-                op0=ALU.is_gt,
-                op1=ALU.mult,
+            words = dz_halves[m][:].rearrange("p r u e -> p r (u e)").bitcast(F32)
+            nc.vector.tensor_copy(
+                out=dz_grp[:].rearrange("p u j -> p (u j)").bitcast(F32).rearrange(
+                    "p (u r) -> p u r", r=PACK // 2
+                ),
+                in_=words.rearrange("p r u -> p u r"),
             )
             dz_grouped[m] = dz_grp
 
@@ -132,6 +147,8 @@ def tile_paralleldense_v_kernel(tc, x, W, b, z, grad_out, out):
         with tc.manual_schedule():
             mask_dz(0)
             mask_dz(1)
+            interleave_dz(0)
+            interleave_dz(1)
             quantise_dz(0)
             quantise_dz(1)
             group_x(0)
@@ -148,6 +165,8 @@ def tile_paralleldense_v_kernel(tc, x, W, b, z, grad_out, out):
             multiply_and_store(1)
             mask_dz(2)
             mask_dz(3)
+            interleave_dz(2)
+            interleave_dz(3)
             group_x(5)
             group_x(6)
             quantise_dz(2)
@@ -155,15 +174,22 @@ def tile_paralleldense_v_kernel(tc, x, W, b, z, grad_out, out):
             multiply_and_store(2)
             multiply_and_store(3)
             mask_dz(4)
+            quantise_x(5)
+            interleave_dz(4)
             mask_dz(5)
             group_x(7)
             quantise_dz(4)
             multiply_and_store(4)
-            quantise_x(5)
+            interleave_dz(5)
+            mask_dz(6)
             quantise_dz(5)
             multiply_and_store(5)
-            for m in (6, 7):
-                mask_dz(m)
-                quantise_x(m)
-                quantise_dz(m)
-                multiply_and_store(m)
+            interleave_dz(6)
+            quantise_x(6)
+            quantise_dz(6)
+            multiply_and_store(6)
+            mask_dz(7)
+            quantise_x(7)
+            interleave_dz(7)
+            quantise_dz(7)
+            multiply_and_store(7)

from contextlib import ExitStack

import concourse.mybir as mybir

F32 = mybir.dt.float32
BF16 = mybir.dt.bfloat16
U32 = mybir.dt.uint32
U8 = mybir.dt.uint8
E4M3_X4 = mybir.dt.float8_e4m3fn_x4
E5M2_X4 = mybir.dt.float8_e5m2_x4
ALU = mybir.AluOpType

P = 128
PACK = 4
BATCH, MASKS, F_IN, U_OUT = 512, 8, 512, 512
assert BATCH == P * PACK
F_TILES = F_IN // P
GROUP = 2
GROUPS = MASKS // GROUP
G_GROUP = 4
STORES = ((0, 2, 0, 4), (2, 2, 0, 4), (4, 1, 0, 4), (5, 1, 0, 4), (6, 1, 0, 4), (7, 1, 0, 2), (7, 1, 2, 2))
X_ON_VECTOR = 3

FLOPS = 2 * MASKS * BATCH * F_IN * U_OUT
BYTES = MASKS * BATCH * (2 * F_IN + 2 * U_OUT + 4 * U_OUT) + 4 * MASKS * F_IN * U_OUT


def tile_paralleldense_v_kernel(tc, x, W, b, z, grad_out, out):
    nc = tc.nc
    x_rows = x.rearrange("(p j) m f -> p j m f", j=PACK)
    z_rows = z.rearrange("(p j) m u -> p j m u", j=PACK)
    g_rows = grad_out.rearrange("(p j) (m u) -> p j m u", j=PACK, m=MASKS)
    out_rows = out.rearrange("m (c t) u -> c m t u", t=F_TILES)

    with ExitStack() as ctx:
        keep = ctx.enter_context(tc.tile_pool(name="keep", bufs=1))
        g_pool = ctx.enter_context(tc.tile_pool(name="g_pool", bufs=MASKS // G_GROUP))
        z_pool = ctx.enter_context(tc.tile_pool(name="z_pool", bufs=GROUPS - 1))
        x_stage = ctx.enter_context(tc.tile_pool(name="x_stage", bufs=4))
        dz_stage = ctx.enter_context(tc.tile_pool(name="dz_stage", bufs=2))
        half_pool = ctx.enter_context(tc.tile_pool(name="half_pool", bufs=2))
        psum = ctx.enter_context(tc.psum_pool(name="psum", bufs=8))

        x_raw = keep.tile([P, PACK, MASKS, F_IN], BF16)
        x_codes = keep.tile([P, MASKS, F_IN], U32, align_bytes=64)
        x_scales = keep.tile([P, MASKS, F_IN], U8, align_bytes=64)
        result = keep.tile([P, MASKS, F_TILES, U_OUT], F32)

        g_raws = []
        z_raws = []
        for h in range(GROUPS):
            pair = slice(h * GROUP, (h + 1) * GROUP)
            if (h * GROUP) % G_GROUP == 0:
                g_raw = g_pool.tile([P, PACK, G_GROUP, U_OUT], BF16)
                nc.sync.dma_start(
                    out=g_raw[:], in_=g_rows[:, :, h * GROUP : h * GROUP + G_GROUP, :]
                )
                g_raws.append(g_raw)
            z_raw = z_pool.tile([P, PACK, GROUP, U_OUT], F32)
            nc.sync.dma_start(out=z_raw[:], in_=z_rows[:, :, pair, :])
            z_raws.append(z_raw)
            if h == 0:
                nc.sync.dma_start(out=x_raw[:], in_=x_rows)

        x_grouped = {}
        dz_halves = {}
        dz_grouped = {}
        dz_quantised = {}

        def group_x(m):
            x_grp = x_stage.tile([P, F_TILES, P, PACK], BF16, align_bytes=64)
            dst = x_grp[:].rearrange("p t c j -> p c j t")
            src = x_raw[:, :, m, :].rearrange("p j (c t) -> p c j t", t=F_TILES)
            if m < X_ON_VECTOR:
                nc.vector.tensor_copy(out=dst, in_=src)
            else:
                nc.scalar.copy(out=dst, in_=src)
            x_grouped[m] = x_grp

        def quantise_x(m):
            nc.vector.quantize_mx(
                out=x_codes[:, m, :].bitcast(E4M3_X4),
                scales=x_scales[:, m, :],
                in_=x_grouped[m][:].rearrange("p t c j -> p (t c j)"),
            )

        def mask_dz(m):
            halves = half_pool.tile([P, PACK // 2, U_OUT, 2], BF16, align_bytes=64)
            for r in range(PACK // 2):
                rows = slice(2 * r, 2 * r + 2)
                nc.vector.scalar_tensor_tensor(
                    out=halves[:, r],
                    in0=z_raws[m // GROUP][:, rows, m % GROUP, :].rearrange("p e u -> p u e"),
                    scalar=0.0,
                    in1=g_raws[m // G_GROUP][:, rows, m % G_GROUP, :].rearrange("p e u -> p u e"),
                    op0=ALU.is_gt,
                    op1=ALU.mult,
                )
            dz_halves[m] = halves

        def interleave_dz(m):
            dz_grp = dz_stage.tile([P, U_OUT, PACK], BF16, align_bytes=64)
            words = dz_halves[m][:].rearrange("p r u e -> p r (u e)").bitcast(F32)
            nc.vector.tensor_copy(
                out=dz_grp[:].rearrange("p u j -> p (u j)").bitcast(F32).rearrange(
                    "p (u r) -> p u r", r=PACK // 2
                ),
                in_=words.rearrange("p r u -> p u r"),
            )
            dz_grouped[m] = dz_grp

        def quantise_dz(m):
            dz_codes = dz_stage.tile([P, U_OUT], U32, align_bytes=64)
            dz_scales = dz_stage.tile([P, U_OUT], U8, align_bytes=64)
            nc.vector.quantize_mx(
                out=dz_codes[:].bitcast(E5M2_X4),
                scales=dz_scales[:],
                in_=dz_grouped[m][:].rearrange("p u j -> p (u j)"),
            )
            dz_quantised[m] = (dz_codes, dz_scales)

        def multiply_and_store(m):
            dz_codes, dz_scales = dz_quantised[m]
            for t in range(F_TILES):
                f_cols = slice(t * P, (t + 1) * P)
                acc = psum.tile([P, U_OUT], F32)
                nc.tensor.matmul_mx(
                    out=acc[:],
                    lhsT=x_codes[:, m, f_cols].bitcast(E4M3_X4),
                    lhsT_scale=x_scales[:, m, f_cols],
                    rhs=dz_codes[:].bitcast(E5M2_X4),
                    rhs_scale=dz_scales[:],
                    start=True,
                    stop=True,
                )
                if m == MASKS - 1 and t % 2 == 0:
                    nc.vector.tensor_copy(out=result[:, m, t, :], in_=acc[:])
                else:
                    nc.scalar.copy(out=result[:, m, t, :], in_=acc[:])
                for m0, n_m, t0, n_t in STORES:
                    if (m, t) == (m0 + n_m - 1, t0 + n_t - 1):
                        nc.sync.dma_start(
                            out=out_rows[:, m0 : m0 + n_m, t0 : t0 + n_t, :],
                            in_=result[:, m0 : m0 + n_m, t0 : t0 + n_t, :],
                        )

        with tc.manual_schedule():
            mask_dz(0)
            mask_dz(1)
            interleave_dz(0)
            interleave_dz(1)
            quantise_dz(0)
            quantise_dz(1)
            group_x(0)
            group_x(3)
            group_x(1)
            group_x(4)
            quantise_x(0)
            group_x(2)
            quantise_x(1)
            quantise_x(3)
            quantise_x(2)
            quantise_x(4)
            multiply_and_store(0)
            multiply_and_store(1)
            mask_dz(2)
            mask_dz(3)
            interleave_dz(2)
            interleave_dz(3)
            group_x(5)
            group_x(6)
            quantise_dz(2)
            quantise_dz(3)
            multiply_and_store(2)
            multiply_and_store(3)
            mask_dz(4)
            quantise_x(5)
            interleave_dz(4)
            mask_dz(5)
            group_x(7)
            quantise_dz(4)
            multiply_and_store(4)
            interleave_dz(5)
            mask_dz(6)
            quantise_dz(5)
            multiply_and_store(5)
            interleave_dz(6)
            quantise_x(6)
            quantise_dz(6)
            multiply_and_store(6)
            mask_dz(7)
            quantise_x(7)
            interleave_dz(7)
            quantise_dz(7)
            multiply_and_store(7)
